import numpy as np
import ml_dtypes


def mxq(x, axis, fmt="e4m3"):
    dtype, down = {"e4m3": (ml_dtypes.float8_e4m3fn, 7), "e5m2": (ml_dtypes.float8_e5m2, 14)}[fmt]
    v = np.moveaxis(np.asarray(x, np.float32).astype(ml_dtypes.bfloat16).astype(np.float64), axis, -1)
    blocks = v.reshape(v.shape[:-1] + (-1, 32))
    amax = np.abs(blocks).max(-1, keepdims=True)
    byte = np.maximum(np.where(amax > 0, np.frexp(amax)[1] - 1 + 127, 0) - down, 1)
    scale = np.exp2(byte - 127.0)
    codes = (blocks / scale).astype(np.float32).astype(dtype).astype(np.float64)
    return np.moveaxis((codes * scale).reshape(v.shape), -1, axis)


WIDE = False


def mx_kscale(k):
    if not WIDE:
        return np.ones(k)
    levels = np.array([10, -10, 5, -5, 0])
    a = np.random.permutation(np.resize(levels, k // 512 * 4)).reshape(k // 512, 4)
    idx = np.arange(k)
    return np.exp2(a[idx // 512, idx % 128 // 32])


BF16 = ml_dtypes.bfloat16


def bf(x):
    return np.asarray(x, np.float32).astype(BF16)


def f64(x):
    return np.asarray(x).astype(np.float64)


E2M1 = np.array([0.0, 0.5, 1.0, 1.5, 2.0, 3.0, 4.0, 6.0, -0.0, -0.5, -1.0, -1.5, -2.0, -3.0, -4.0, -6.0])


def pack_weight(w, fmt):
    k, n = w.shape
    w = f64(bf(w)).reshape(k // 32, 32, n)
    amax = np.abs(w).max(1)
    if fmt == "e4m3":
        byte = np.frexp(amax)[1] - 1 + 127 - 7
    else:
        mant, ex = np.frexp(amax / 6.0)
        byte = np.where(mant > 0.5, ex, ex - 1) + 127
    byte = np.clip(np.where(amax > 0, byte, 1), 1, 254)
    scaled = (w * np.exp2(127.0 - byte)[:, None, :]).reshape(k, n).astype(np.float32)
    by_word = np.ascontiguousarray(scaled.reshape(k // 512, 128, 4, n).transpose(0, 1, 3, 2))
    if fmt == "e4m3":
        words = by_word.astype(ml_dtypes.float8_e4m3fn).view(np.uint8)
    else:
        c = by_word.astype(ml_dtypes.float4_e2m1fn).view(np.uint8) & 0xF
        words = c[..., 0::2] | (c[..., 1::2] << 4)
    return np.ascontiguousarray(words), np.ascontiguousarray(byte.astype(np.uint8).reshape(k // 512, 16, n))


def unpack_weight(words, scales, fmt):
    g, p, n, _ = words.shape
    if fmt == "e4m3":
        vals = np.ascontiguousarray(words).view(ml_dtypes.float8_e4m3fn).astype(np.float64)
    else:
        nib = np.empty((g, p, n, 4), np.uint8)
        nib[..., 0::2] = words & 0xF
        nib[..., 1::2] = words >> 4
        vals = E2M1[nib]
    vals = vals * np.repeat(np.exp2(scales.astype(np.float64) - 127.0), 8, axis=1)[..., None]
    return vals.transpose(0, 1, 3, 2).reshape(g * 512, n)


B, T, D, H, HD, Q_STRIDE, WINDOW, QKV = 1, 1536, 1024, 16, 64, 4, 128, 3
NW = T // (Q_STRIDE * WINDOW)
SEQ = T // NW
FMT = "e4m3"


def setup_inputs():
    s = mx_kscale(SEQ)
    t = mx_kscale(D)
    g = np.exp(np.random.standard_normal((B, H, NW, SEQ // Q_STRIDE, SEQ)) * 1.3)
    vd = np.random.standard_normal((B, NW, SEQ, D)) * t / s[:, None]
    w = np.random.standard_normal((D, D)) * 5.0 / np.sqrt(D) / t[None, :]
    words, scales = pack_weight(np.ascontiguousarray(w.T), FMT)
    return {"attn": bf(g / g.sum(-1, keepdims=True) * s),
            "v": bf(np.ascontiguousarray(vd.reshape(B, NW, SEQ, H, HD).transpose(0, 3, 1, 2, 4))),
            "proj_w_words": words,
            "proj_w_scales": scales,
            "proj_b": bf(np.random.standard_normal(D) * 0.2)}


def reference(attn, v, proj_w_words, proj_w_scales, proj_b):
    o = mxq(f64(attn), 4, "e4m3") @ mxq(f64(v), 3, "e4m3")
    o = o.transpose(0, 3, 2, 1, 4).reshape(B, -1, H * HD)
    return (mxq(o, 2, "e4m3") @ unpack_weight(proj_w_words, proj_w_scales, FMT)) + f64(proj_b)

@@ -1,0 +1,225 @@
+from contextlib import ExitStack
+
+import concourse.mybir as mybir
+from concourse.masks import make_identity
+
+BF16 = mybir.dt.bfloat16
+F32 = mybir.dt.float32
+I32 = mybir.dt.int32
+U32 = mybir.dt.uint32
+U8 = mybir.dt.uint8
+FP8X4 = mybir.dt.float8_e4m3fn_x4
+
+P = 128
+PACK = 4
+HEADS = 16
+WINDOWS = 3
+QUERIES = 128
+KEYS = 512
+HEAD_DIM = 64
+CHANNELS = HEADS * HEAD_DIM
+K_PASS = P * PACK
+PASSES = CHANNELS // K_PASS
+N_TILE = 512
+N_TILES = CHANNELS // N_TILE
+
+GROUP_HEADS = 4
+GROUPS_PER_WINDOW = HEADS // GROUP_HEADS
+GROUPS = WINDOWS * GROUPS_PER_WINDOW
+GROUPS_PER_HALF = K_PASS // (GROUP_HEADS * HEAD_DIM)
+QUERY_RUN = 4
+QUERY_RUNS = QUERIES // QUERY_RUN
+KEY_WORDS = KEYS // 2
+WORD_PLANES = 2
+
+FLOPS = 2 * HEADS * WINDOWS * QUERIES * KEYS * HEAD_DIM + 2 * WINDOWS * QUERIES * CHANNELS * CHANNELS
+
+
+def tile_hieramaskunitattention_pb_kernel(tc, attn, v, proj_w_words, proj_w_scales, proj_b, out):
+    nc = tc.nc
+    with ExitStack() as ctx:
+        ctx.enter_context(tc.manual_schedule())
+        const = ctx.enter_context(tc.tile_pool(name="const", bufs=1))
+        loads = ctx.enter_context(tc.tile_pool(name="loads", bufs=GROUPS))
+        stage = ctx.enter_context(tc.tile_pool(name="stage", bufs=3))
+        results = ctx.enter_context(tc.tile_pool(name="results", bufs=WINDOWS * N_TILES))
+        psum_attn = ctx.enter_context(tc.psum_pool(name="psum_attn", bufs=4))
+        psum_mixed = ctx.enter_context(tc.psum_pool(name="psum_mixed", bufs=1))
+        psum_merged = ctx.enter_context(tc.psum_pool(name="psum_merged", bufs=1))
+        psum_out = ctx.enter_context(tc.psum_pool(name="psum_out", bufs=N_TILES))
+
+        ident_f32 = const.tile([P, P], F32)
+        make_identity(nc, ident_f32[:])
+        ident_bf16 = const.tile([P, P], BF16)
+        make_identity(nc, ident_bf16[:])
+
+        w_scales = const.tile([P, PASSES, CHANNELS], U8, align_bytes=64)
+        nc.vector.memset(w_scales[:].bitcast(I32), 0)
+
+        bias_rows = const.tile([P, CHANNELS], BF16)
+        nc.vector.memset(bias_rows[:], 0.0)
+        ones = const.tile([P, P], BF16)
+        nc.vector.memset(ones[:], 1.0)
+
+        attn_rows = []
+        v_rows = []
+        w_words = const.tile([P, PASSES, CHANNELS * PACK], U8, align_bytes=64)
+        for i in range(GROUPS):
+            w, first_head = i // GROUPS_PER_WINDOW, GROUP_HEADS * (i % GROUPS_PER_WINDOW)
+            heads = slice(first_head, first_head + GROUP_HEADS)
+            attn_in = loads.tile([P, QUERY_RUN * KEYS], BF16)
+            nc.sync.dma_start(
+                out=attn_in[:],
+                in_=attn[0, heads, w].rearrange("h (r j) k -> r h (j k)", j=QUERY_RUN),
+            )
+            attn_rows.append(attn_in)
+            v_in = loads.tile([P, GROUP_HEADS, PACK * HEAD_DIM], BF16)
+            nc.sync.dma_start(out=v_in[:], in_=v[0, heads, w].rearrange("h (p t) d -> p h (t d)", t=PACK))
+            v_rows.append(v_in)
+            if i == 0:
+                for quadrant in range(4):
+                    nc.sync.dma_start(
+                        out=w_scales[32 * quadrant : 32 * quadrant + 4].bitcast(I32),
+                        in_=proj_w_scales[:, 4 * quadrant : 4 * quadrant + 4, :].rearrange("g r n -> r g n").bitcast(I32),
+                    )
+                nc.sync.dma_start(out=bias_rows[0:1, :], in_=proj_b.unsqueeze(0))
+            if i == GROUPS_PER_WINDOW - 1:
+                nc.sync.dma_start(
+                    out=w_words[:].bitcast(I32),
+                    in_=proj_w_words.rearrange("g p n t -> p g (n t)").bitcast(I32),
+                )
+
+        bias_all = const.tile([P, CHANNELS], F32)
+
+        def spread_bias():
+            for n in range(N_TILES):
+                cols = slice(n * N_TILE, (n + 1) * N_TILE)
+                spread = psum_out.tile([P, N_TILE], F32, tag="out_bank")
+                nc.tensor.matmul(out=spread[:], lhsT=ones[:], rhs=bias_rows[:, cols], start=True, stop=True)
+                nc.vector.tensor_copy(out=bias_all[:, cols], in_=spread[:])
+
+        out_rows = out[0].rearrange("(q w) n -> w q n", w=WINDOWS)
+
+        attn_grouped = {}
+        attn_mx = {}
+        v_grouped = {}
+        v_mx = {}
+        mixed = {}
+        merged_rows = {}
+        merged_mx = {}
+        out_banks = {}
+
+        def transpose_attn(i):
+            words = attn_rows[i][:].bitcast(F32)
+            grouped = stage.tile([P, GROUP_HEADS * QUERIES * PACK], BF16, align_bytes=64, name="attn_grouped")
+            grouped_words = grouped[:].bitcast(F32).rearrange(
+                "p (h r b ju) -> p b h r ju", h=GROUP_HEADS, r=QUERY_RUNS, b=2
+            )
+            for b in range(2):
+                flipped = psum_attn.tile([P, 2, WORD_PLANES, P], F32)
+                for j in range(2):
+                    first = (2 * b + j) * KEY_WORDS
+                    for u in range(WORD_PLANES):
+                        nc.tensor.transpose(
+                            flipped[:, j, u, :], words[:, first + u : first + KEY_WORDS : WORD_PLANES], ident_f32[:]
+                        )
+                nc.scalar.copy(
+                    out=grouped_words[:, b], in_=flipped[:].rearrange("p j u (r h) -> p h r (j u)", h=GROUP_HEADS)
+                )
+            attn_grouped[i] = grouped
+
+        def quantise(grouped, width, name):
+            codes = stage.tile([P, width], U32, align_bytes=64, name=name + "_codes")
+            scales = stage.tile([P, width], U8, align_bytes=64, name=name + "_scales")
+            nc.vector.quantize_mx(out=codes[:].bitcast(FP8X4), scales=scales[:], in_=grouped[:])
+            return codes, scales
+
+        def regroup_v(i):
+            grouped = stage.tile([P, GROUP_HEADS * HEAD_DIM * PACK], BF16, align_bytes=64, name="v_grouped")
+            nc.vector.tensor_copy(
+                out=grouped[:].rearrange("p (h d t) -> p h d t", h=GROUP_HEADS, t=PACK),
+                in_=v_rows[i][:].rearrange("p h (t d) -> p h d t", t=PACK),
+            )
+            v_grouped[i] = grouped
+
+        def mix_values(i):
+            half, place = i // GROUPS_PER_HALF, i % GROUPS_PER_HALF
+            if place == 0:
+                mixed[half] = psum_mixed.tile([P, K_PASS], F32, name="mixed")
+            a_codes, a_scales = attn_mx[i]
+            v_codes, v_scales = v_mx[i]
+            for h in range(GROUP_HEADS):
+                q_cols = slice(h * QUERIES, (h + 1) * QUERIES)
+                d_cols = slice(h * HEAD_DIM, (h + 1) * HEAD_DIM)
+                first = (place * GROUP_HEADS + h) * HEAD_DIM
+                nc.tensor.matmul_mx(
+                    out=mixed[half][:, first : first + HEAD_DIM],
+                    lhsT=a_codes[:, q_cols].bitcast(FP8X4),
+                    lhsT_scale=a_scales[:, q_cols],
+                    rhs=v_codes[:, d_cols].bitcast(FP8X4),
+                    rhs_scale=v_scales[:, d_cols],
+                    start=True,
+                    stop=True,
+                )
+
+        def round_mixed(half):
+            rows = stage.tile([P, PACK, P], BF16, name="merged_rows")
+            nc.scalar.copy(out=rows[:], in_=mixed[half][:].rearrange("p (c t) -> p t c", t=PACK))
+            merged_rows[half] = rows
+
+        def transpose_merged(half):
+            flipped = psum_merged.tile([P, PACK, P], BF16, name="merged_flipped")
+            for t in range(PACK):
+                nc.tensor.transpose(flipped[:, t, :], merged_rows[half][:, t, :], ident_bf16[:])
+            grouped = stage.tile([P, QUERIES * PACK], BF16, align_bytes=64, name="merged_grouped")
+            nc.scalar.copy(
+                out=grouped[:].rearrange("p (q t) -> p q t", t=PACK), in_=flipped[:].rearrange("p t q -> p q t")
+            )
+            return grouped
+
+        def project(half):
+            w, g = half // PASSES, half % PASSES
+            m_codes, m_scales = merged_mx[half]
+            for n in range(N_TILES):
+                if g == 0:
+                    out_banks[n] = psum_out.tile([P, N_TILE], F32, tag="out_bank", name="out_bank")
+                nc.tensor.matmul_mx(
+                    out=out_banks[n][:],
+                    lhsT=m_codes[:].bitcast(FP8X4),
+                    lhsT_scale=m_scales[:],
+                    rhs=w_words[:, g, n * N_TILE * PACK : (n + 1) * N_TILE * PACK].bitcast(FP8X4),
+                    rhs_scale=w_scales[:, g, n * N_TILE : (n + 1) * N_TILE],
+                    start=(g == 0),
+                    stop=(g == PASSES - 1),
+                )
+            if g == PASSES - 1:
+                for n in range(N_TILES):
+                    cols = slice(n * N_TILE, (n + 1) * N_TILE)
+                    result = results.tile([P, N_TILE], F32)
+                    nc.vector.tensor_add(out=result[:], in0=out_banks[n][:], in1=bias_all[:, cols])
+                    nc.sync.dma_start(out=out_rows[w][:, cols], in_=result[:])
+
+        def closes_half(i):
+            return 0 <= i < GROUPS and i % GROUPS_PER_HALF == GROUPS_PER_HALF - 1
+
+        def step(i):
+            if i < GROUPS:
+                regroup_v(i)
+            if closes_half(i - 2):
+                half = (i - 2) // GROUPS_PER_HALF
+                merged_mx[half] = quantise(transpose_merged(half), QUERIES, "merged")
+            if i < GROUPS:
+                transpose_attn(i)
+                attn_mx[i] = quantise(attn_grouped[i], GROUP_HEADS * QUERIES, "attn")
+                v_mx[i] = quantise(v_grouped[i], GROUP_HEADS * HEAD_DIM, "v")
+            if 0 <= i - 1 < GROUPS:
+                mix_values(i - 1)
+            if closes_half(i - 1):
+                round_mixed((i - 1) // GROUPS_PER_HALF)
+            if closes_half(i - 3):
+                project((i - 3) // GROUPS_PER_HALF)
+
+        step(0)
+        spread_bias()
+        for i in range(1, GROUPS + 3):
+            step(i)

@@ -106,6 +106,7 @@ def tile_hieramaskunitattention_pb_kernel(tc, attn, v, proj_w_words, proj_w_scal
         v_mx = {}
         mixed = {}
         merged_rows = {}
+        merged_grouped = {}
         merged_mx = {}
         out_banks = {}
 
@@ -175,10 +176,10 @@ def tile_hieramaskunitattention_pb_kernel(tc, attn, v, proj_w_words, proj_w_scal
             nc.scalar.copy(
                 out=grouped[:].rearrange("p (q t) -> p q t", t=PACK), in_=flipped[:].rearrange("p t q -> p q t")
             )
-            return grouped
+            merged_grouped[half] = grouped
 
         def project(half):
-            w, g = half // PASSES, half % PASSES
+            g = half % PASSES
             m_codes, m_scales = merged_mx[half]
             for n in range(N_TILES):
                 if g == 0:
@@ -192,34 +193,44 @@ def tile_hieramaskunitattention_pb_kernel(tc, attn, v, proj_w_words, proj_w_scal
                     start=(g == 0),
                     stop=(g == PASSES - 1),
                 )
-            if g == PASSES - 1:
-                for n in range(N_TILES):
-                    cols = slice(n * N_TILE, (n + 1) * N_TILE)
-                    result = results.tile([P, N_TILE], F32)
-                    nc.vector.tensor_add(out=result[:], in0=out_banks[n][:], in1=bias_all[:, cols])
-                    nc.sync.dma_start(out=out_rows[w][:, cols], in_=result[:])
 
-        def closes_half(i):
-            return 0 <= i < GROUPS and i % GROUPS_PER_HALF == GROUPS_PER_HALF - 1
+        def finish_window(w):
+            for n in range(N_TILES):
+                cols = slice(n * N_TILE, (n + 1) * N_TILE)
+                result = results.tile([P, N_TILE], F32)
+                nc.vector.tensor_add(out=result[:], in0=out_banks[n][:], in1=bias_all[:, cols])
+                nc.sync.dma_start(out=out_rows[w][:, cols], in_=result[:])
+
+        def half_closed_by(j):
+            if 0 <= j < GROUPS and j % GROUPS_PER_HALF == GROUPS_PER_HALF - 1:
+                return j // GROUPS_PER_HALF
+            return None
 
         def step(i):
-            if i < GROUPS:
-                regroup_v(i)
-            if closes_half(i - 2):
-                half = (i - 2) // GROUPS_PER_HALF
-                merged_mx[half] = quantise(transpose_merged(half), QUERIES, "merged")
+            to_transpose = half_closed_by(i - 3)
+            to_project = half_closed_by(i - 4)
+            to_finish = half_closed_by(i - 5)
+            if to_transpose is not None:
+                round_mixed(to_transpose)
+            if 0 <= i - 1 < GROUPS:
+                attn_mx[i - 1] = quantise(attn_grouped[i - 1], GROUP_HEADS * QUERIES, "attn")
+            if to_project is not None:
+                merged_mx[to_project] = quantise(merged_grouped[to_project], QUERIES, "merged")
             if i < GROUPS:
                 transpose_attn(i)
-                attn_mx[i] = quantise(attn_grouped[i], GROUP_HEADS * QUERIES, "attn")
+                regroup_v(i)
+            if to_transpose is not None:
+                transpose_merged(to_transpose)
+            if to_finish is not None and to_finish % PASSES == PASSES - 1:
+                finish_window(to_finish // PASSES)
+            if i < GROUPS:
                 v_mx[i] = quantise(v_grouped[i], GROUP_HEADS * HEAD_DIM, "v")
-            if 0 <= i - 1 < GROUPS:
-                mix_values(i - 1)
-            if closes_half(i - 1):
-                round_mixed((i - 1) // GROUPS_PER_HALF)
-            if closes_half(i - 3):
-                project((i - 3) // GROUPS_PER_HALF)
+            if 0 <= i - 2 < GROUPS:
+                mix_values(i - 2)
+            if to_project is not None:
+                project(to_project)
 
         step(0)
         spread_bias()
-        for i in range(1, GROUPS + 3):
+        for i in range(1, GROUPS + 5):
             step(i)

@@ -43,10 +43,10 @@ def tile_hieramaskunitattention_pb_kernel(tc, attn, v, proj_w_words, proj_w_scal
         loads = ctx.enter_context(tc.tile_pool(name="loads", bufs=GROUPS))
         stage = ctx.enter_context(tc.tile_pool(name="stage", bufs=3))
         results = ctx.enter_context(tc.tile_pool(name="results", bufs=WINDOWS * N_TILES))
-        psum_attn = ctx.enter_context(tc.psum_pool(name="psum_attn", bufs=4))
+        kept = ctx.enter_context(tc.tile_pool(name="kept", bufs=WINDOWS * PASSES))
         psum_mixed = ctx.enter_context(tc.psum_pool(name="psum_mixed", bufs=1))
         psum_merged = ctx.enter_context(tc.psum_pool(name="psum_merged", bufs=1))
-        psum_out = ctx.enter_context(tc.psum_pool(name="psum_out", bufs=N_TILES))
+        psum_turns = ctx.enter_context(tc.psum_pool(name="psum_turns", bufs=WINDOWS * N_TILES))
 
         ident_f32 = const.tile([P, P], F32)
         make_identity(nc, ident_f32[:])
@@ -83,18 +83,17 @@ def tile_hieramaskunitattention_pb_kernel(tc, attn, v, proj_w_words, proj_w_scal
                         in_=proj_w_scales[:, 4 * quadrant : 4 * quadrant + 4, :].rearrange("g r n -> r g n").bitcast(I32),
                     )
                 nc.sync.dma_start(out=bias_rows[0:1, :], in_=proj_b.unsqueeze(0))
-            if i == GROUPS_PER_WINDOW - 1:
-                nc.sync.dma_start(
-                    out=w_words[:].bitcast(I32),
-                    in_=proj_w_words.rearrange("g p n t -> p g (n t)").bitcast(I32),
-                )
+        nc.sync.dma_start(
+            out=w_words[:].bitcast(I32),
+            in_=proj_w_words.rearrange("g p n t -> p g (n t)").bitcast(I32),
+        )
 
         bias_all = const.tile([P, CHANNELS], F32)
 
         def spread_bias():
             for n in range(N_TILES):
                 cols = slice(n * N_TILE, (n + 1) * N_TILE)
-                spread = psum_out.tile([P, N_TILE], F32, tag="out_bank")
+                spread = psum_turns.tile([P, N_TILE], F32, tag="turn")
                 nc.tensor.matmul(out=spread[:], lhsT=ones[:], rhs=bias_rows[:, cols], start=True, stop=True)
                 nc.vector.tensor_copy(out=bias_all[:, cols], in_=spread[:])
 
@@ -117,7 +116,7 @@ def tile_hieramaskunitattention_pb_kernel(tc, attn, v, proj_w_words, proj_w_scal
                 "p (h r b ju) -> p b h r ju", h=GROUP_HEADS, r=QUERY_RUNS, b=2
             )
             for b in range(2):
-                flipped = psum_attn.tile([P, 2, WORD_PLANES, P], F32)
+                flipped = psum_turns.tile([P, 2, WORD_PLANES, P], F32, tag="turn")
                 for j in range(2):
                     first = (2 * b + j) * KEY_WORDS
                     for u in range(WORD_PLANES):
@@ -129,9 +128,9 @@ def tile_hieramaskunitattention_pb_kernel(tc, attn, v, proj_w_words, proj_w_scal
                 )
             attn_grouped[i] = grouped
 
-        def quantise(grouped, width, name):
-            codes = stage.tile([P, width], U32, align_bytes=64, name=name + "_codes")
-            scales = stage.tile([P, width], U8, align_bytes=64, name=name + "_scales")
+        def quantise(pool, grouped, width, name):
+            codes = pool.tile([P, width], U32, align_bytes=64, name=name + "_codes")
+            scales = pool.tile([P, width], U8, align_bytes=64, name=name + "_scales")
             nc.vector.quantize_mx(out=codes[:].bitcast(FP8X4), scales=scales[:], in_=grouped[:])
             return codes, scales
 
@@ -178,28 +177,29 @@ def tile_hieramaskunitattention_pb_kernel(tc, attn, v, proj_w_words, proj_w_scal
             )
             merged_grouped[half] = grouped
 
-        def project(half):
-            g = half % PASSES
-            m_codes, m_scales = merged_mx[half]
+        def project_window(w):
             for n in range(N_TILES):
-                if g == 0:
-                    out_banks[n] = psum_out.tile([P, N_TILE], F32, tag="out_bank", name="out_bank")
-                nc.tensor.matmul_mx(
-                    out=out_banks[n][:],
-                    lhsT=m_codes[:].bitcast(FP8X4),
-                    lhsT_scale=m_scales[:],
-                    rhs=w_words[:, g, n * N_TILE * PACK : (n + 1) * N_TILE * PACK].bitcast(FP8X4),
-                    rhs_scale=w_scales[:, g, n * N_TILE : (n + 1) * N_TILE],
-                    start=(g == 0),
-                    stop=(g == PASSES - 1),
-                )
+                out_banks[w, n] = psum_turns.tile([P, N_TILE], F32, tag="turn", name="out_bank")
+                for g in range(PASSES):
+                    m_codes, m_scales = merged_mx[w * PASSES + g]
+                    nc.tensor.matmul_mx(
+                        out=out_banks[w, n][:],
+                        lhsT=m_codes[:].bitcast(FP8X4),
+                        lhsT_scale=m_scales[:],
+                        rhs=w_words[:, g, n * N_TILE * PACK : (n + 1) * N_TILE * PACK].bitcast(FP8X4),
+                        rhs_scale=w_scales[:, g, n * N_TILE : (n + 1) * N_TILE],
+                        start=(g == 0),
+                        stop=(g == PASSES - 1),
+                    )
 
         def finish_window(w):
             for n in range(N_TILES):
                 cols = slice(n * N_TILE, (n + 1) * N_TILE)
                 result = results.tile([P, N_TILE], F32)
-                nc.vector.tensor_add(out=result[:], in0=out_banks[n][:], in1=bias_all[:, cols])
+                nc.vector.tensor_add(out=result[:], in0=out_banks[w, n][:], in1=bias_all[:, cols])
                 nc.sync.dma_start(out=out_rows[w][:, cols], in_=result[:])
+
+        FIRST_PROJECTION = GROUPS + 1
 
         def half_closed_by(j):
             if 0 <= j < GROUPS and j % GROUPS_PER_HALF == GROUPS_PER_HALF - 1:
@@ -208,29 +208,28 @@ def tile_hieramaskunitattention_pb_kernel(tc, attn, v, proj_w_words, proj_w_scal
 
         def step(i):
             to_transpose = half_closed_by(i - 3)
-            to_project = half_closed_by(i - 4)
-            to_finish = half_closed_by(i - 5)
+            to_quantise = half_closed_by(i - 4)
             if to_transpose is not None:
                 round_mixed(to_transpose)
             if 0 <= i - 1 < GROUPS:
-                attn_mx[i - 1] = quantise(attn_grouped[i - 1], GROUP_HEADS * QUERIES, "attn")
-            if to_project is not None:
-                merged_mx[to_project] = quantise(merged_grouped[to_project], QUERIES, "merged")
+                attn_mx[i - 1] = quantise(stage, attn_grouped[i - 1], GROUP_HEADS * QUERIES, "attn")
+            if to_quantise is not None:
+                merged_mx[to_quantise] = quantise(kept, merged_grouped[to_quantise], QUERIES, "merged")
             if i < GROUPS:
                 transpose_attn(i)
                 regroup_v(i)
             if to_transpose is not None:
                 transpose_merged(to_transpose)
-            if to_finish is not None and to_finish % PASSES == PASSES - 1:
-                finish_window(to_finish // PASSES)
+            if 0 <= i - FIRST_PROJECTION - 1 < WINDOWS:
+                finish_window(i - FIRST_PROJECTION - 1)
             if i < GROUPS:
-                v_mx[i] = quantise(v_grouped[i], GROUP_HEADS * HEAD_DIM, "v")
+                v_mx[i] = quantise(stage, v_grouped[i], GROUP_HEADS * HEAD_DIM, "v")
             if 0 <= i - 2 < GROUPS:
                 mix_values(i - 2)
-            if to_project is not None:
-                project(to_project)
+            if 0 <= i - FIRST_PROJECTION < WINDOWS:
+                project_window(i - FIRST_PROJECTION)
 
         step(0)
         spread_bias()
-        for i in range(1, GROUPS + 5):
+        for i in range(1, FIRST_PROJECTION + WINDOWS + 1):
             step(i)

@@ -41,7 +41,7 @@ def tile_hieramaskunitattention_pb_kernel(tc, attn, v, proj_w_words, proj_w_scal
         ctx.enter_context(tc.manual_schedule())
         const = ctx.enter_context(tc.tile_pool(name="const", bufs=1))
         loads = ctx.enter_context(tc.tile_pool(name="loads", bufs=GROUPS))
-        stage = ctx.enter_context(tc.tile_pool(name="stage", bufs=3))
+        stage = ctx.enter_context(tc.tile_pool(name="stage", bufs=4))
         results = ctx.enter_context(tc.tile_pool(name="results", bufs=WINDOWS * N_TILES))
         kept = ctx.enter_context(tc.tile_pool(name="kept", bufs=WINDOWS * PASSES))
         psum_mixed = ctx.enter_context(tc.psum_pool(name="psum_mixed", bufs=1))
@@ -180,8 +180,9 @@ def tile_hieramaskunitattention_pb_kernel(tc, attn, v, proj_w_words, proj_w_scal
         def project_window(w):
             for n in range(N_TILES):
                 out_banks[w, n] = psum_turns.tile([P, N_TILE], F32, tag="turn", name="out_bank")
-                for g in range(PASSES):
-                    m_codes, m_scales = merged_mx[w * PASSES + g]
+            for g in range(PASSES):
+                m_codes, m_scales = merged_mx[w * PASSES + g]
+                for n in range(N_TILES):
                     nc.tensor.matmul_mx(
                         out=out_banks[w, n][:],
                         lhsT=m_codes[:].bitcast(FP8X4),
@@ -207,6 +208,7 @@ def tile_hieramaskunitattention_pb_kernel(tc, attn, v, proj_w_words, proj_w_scal
             return None
 
         def step(i):
+            to_mix = half_closed_by(i - 2)
             to_transpose = half_closed_by(i - 3)
             to_quantise = half_closed_by(i - 4)
             if to_transpose is not None:
@@ -224,8 +226,9 @@ def tile_hieramaskunitattention_pb_kernel(tc, attn, v, proj_w_words, proj_w_scal
                 finish_window(i - FIRST_PROJECTION - 1)
             if i < GROUPS:
                 v_mx[i] = quantise(stage, v_grouped[i], GROUP_HEADS * HEAD_DIM, "v")
-            if 0 <= i - 2 < GROUPS:
-                mix_values(i - 2)
+            if to_mix is not None:
+                for j in range(to_mix * GROUPS_PER_HALF, (to_mix + 1) * GROUPS_PER_HALF):
+                    mix_values(j)
             if 0 <= i - FIRST_PROJECTION < WINDOWS:
                 project_window(i - FIRST_PROJECTION)
 

@@ -27,6 +27,7 @@ GROUP_HEADS = 4
 GROUPS_PER_WINDOW = HEADS // GROUP_HEADS
 GROUPS = WINDOWS * GROUPS_PER_WINDOW
 GROUPS_PER_HALF = K_PASS // (GROUP_HEADS * HEAD_DIM)
+HALVES = WINDOWS * PASSES
 QUERY_RUN = 4
 QUERY_RUNS = QUERIES // QUERY_RUN
 KEY_WORDS = KEYS // 2
@@ -43,7 +44,7 @@ def tile_hieramaskunitattention_pb_kernel(tc, attn, v, proj_w_words, proj_w_scal
         loads = ctx.enter_context(tc.tile_pool(name="loads", bufs=GROUPS))
         stage = ctx.enter_context(tc.tile_pool(name="stage", bufs=4))
         results = ctx.enter_context(tc.tile_pool(name="results", bufs=WINDOWS * N_TILES))
-        kept = ctx.enter_context(tc.tile_pool(name="kept", bufs=WINDOWS * PASSES))
+        kept = ctx.enter_context(tc.tile_pool(name="kept", bufs=HALVES))
         psum_mixed = ctx.enter_context(tc.psum_pool(name="psum_mixed", bufs=1))
         psum_merged = ctx.enter_context(tc.psum_pool(name="psum_merged", bufs=1))
         psum_turns = ctx.enter_context(tc.psum_pool(name="psum_turns", bufs=WINDOWS * N_TILES))
@@ -64,18 +65,30 @@ def tile_hieramaskunitattention_pb_kernel(tc, attn, v, proj_w_words, proj_w_scal
         attn_rows = []
         v_rows = []
         w_words = const.tile([P, PASSES, CHANNELS * PACK], U8, align_bytes=64)
-        for i in range(GROUPS):
-            w, first_head = i // GROUPS_PER_WINDOW, GROUP_HEADS * (i % GROUPS_PER_WINDOW)
-            heads = slice(first_head, first_head + GROUP_HEADS)
-            attn_in = loads.tile([P, QUERY_RUN * KEYS], BF16)
+
+        def window_and_heads(i):
+            first_head = GROUP_HEADS * (i % GROUPS_PER_WINDOW)
+            return i // GROUPS_PER_WINDOW, slice(first_head, first_head + GROUP_HEADS)
+
+        def load_attn(i):
+            w, heads = window_and_heads(i)
+            attn_in = loads.tile([P, QUERY_RUN * KEYS], BF16, name="attn_in")
             nc.sync.dma_start(
                 out=attn_in[:],
                 in_=attn[0, heads, w].rearrange("h (r j) k -> r h (j k)", j=QUERY_RUN),
             )
             attn_rows.append(attn_in)
-            v_in = loads.tile([P, GROUP_HEADS, PACK * HEAD_DIM], BF16)
+
+        def load_v(i):
+            w, heads = window_and_heads(i)
+            v_in = loads.tile([P, GROUP_HEADS, PACK * HEAD_DIM], BF16, name="v_in")
             nc.sync.dma_start(out=v_in[:], in_=v[0, heads, w].rearrange("h (p t) d -> p h (t d)", t=PACK))
             v_rows.append(v_in)
+
+        for i in range(GROUPS):
+            load_attn(i)
+            if i > 0:
+                load_v(i - 1)
             if i == 0:
                 for quadrant in range(4):
                     nc.sync.dma_start(
@@ -83,19 +96,20 @@ def tile_hieramaskunitattention_pb_kernel(tc, attn, v, proj_w_words, proj_w_scal
                         in_=proj_w_scales[:, 4 * quadrant : 4 * quadrant + 4, :].rearrange("g r n -> r g n").bitcast(I32),
                     )
                 nc.sync.dma_start(out=bias_rows[0:1, :], in_=proj_b.unsqueeze(0))
+        load_v(GROUPS - 1)
         nc.sync.dma_start(
             out=w_words[:].bitcast(I32),
             in_=proj_w_words.rearrange("g p n t -> p g (n t)").bitcast(I32),
         )
 
-        bias_all = const.tile([P, CHANNELS], F32)
+        bias_all = const.tile([P, CHANNELS], BF16)
 
         def spread_bias():
+            spread = psum_turns.tile([P, CHANNELS], BF16, tag="turn", name="spread")
             for n in range(N_TILES):
                 cols = slice(n * N_TILE, (n + 1) * N_TILE)
-                spread = psum_turns.tile([P, N_TILE], F32, tag="turn")
-                nc.tensor.matmul(out=spread[:], lhsT=ones[:], rhs=bias_rows[:, cols], start=True, stop=True)
-                nc.vector.tensor_copy(out=bias_all[:, cols], in_=spread[:])
+                nc.tensor.matmul(out=spread[:, cols], lhsT=ones[:], rhs=bias_rows[:, cols], start=True, stop=True)
+            nc.vector.tensor_copy(out=bias_all[:], in_=spread[:])
 
         out_rows = out[0].rearrange("(q w) n -> w q n", w=WINDOWS)
 
@@ -177,21 +191,21 @@ def tile_hieramaskunitattention_pb_kernel(tc, attn, v, proj_w_words, proj_w_scal
             )
             merged_grouped[half] = grouped
 
-        def project_window(w):
-            for n in range(N_TILES):
-                out_banks[w, n] = psum_turns.tile([P, N_TILE], F32, tag="turn", name="out_bank")
-            for g in range(PASSES):
-                m_codes, m_scales = merged_mx[w * PASSES + g]
+        def project(w, g):
+            if g == 0:
                 for n in range(N_TILES):
-                    nc.tensor.matmul_mx(
-                        out=out_banks[w, n][:],
-                        lhsT=m_codes[:].bitcast(FP8X4),
-                        lhsT_scale=m_scales[:],
-                        rhs=w_words[:, g, n * N_TILE * PACK : (n + 1) * N_TILE * PACK].bitcast(FP8X4),
-                        rhs_scale=w_scales[:, g, n * N_TILE : (n + 1) * N_TILE],
-                        start=(g == 0),
-                        stop=(g == PASSES - 1),
-                    )
+                    out_banks[w, n] = psum_turns.tile([P, N_TILE], F32, tag="turn", name="out_bank")
+            m_codes, m_scales = merged_mx[w * PASSES + g]
+            for n in range(N_TILES):
+                nc.tensor.matmul_mx(
+                    out=out_banks[w, n][:],
+                    lhsT=m_codes[:].bitcast(FP8X4),
+                    lhsT_scale=m_scales[:],
+                    rhs=w_words[:, g, n * N_TILE * PACK : (n + 1) * N_TILE * PACK].bitcast(FP8X4),
+                    rhs_scale=w_scales[:, g, n * N_TILE : (n + 1) * N_TILE],
+                    start=(g == 0),
+                    stop=(g == PASSES - 1),
+                )
 
         def finish_window(w):
             for n in range(N_TILES):
@@ -200,39 +214,52 @@ def tile_hieramaskunitattention_pb_kernel(tc, attn, v, proj_w_words, proj_w_scal
                 nc.vector.tensor_add(out=result[:], in0=out_banks[w, n][:], in1=bias_all[:, cols])
                 nc.sync.dma_start(out=out_rows[w][:, cols], in_=result[:])
 
-        FIRST_PROJECTION = GROUPS + 1
+        def quantise_group(i):
+            attn_mx[i] = quantise(stage, attn_grouped[i], GROUP_HEADS * QUERIES, "attn")
+
+        def quantise_v(i):
+            v_mx[i] = quantise(stage, v_grouped[i], GROUP_HEADS * HEAD_DIM, "v")
+
+        def quantise_merged(half):
+            merged_mx[half] = quantise(kept, merged_grouped[half], QUERIES, "merged")
 
         def half_closed_by(j):
             if 0 <= j < GROUPS and j % GROUPS_PER_HALF == GROUPS_PER_HALF - 1:
                 return j // GROUPS_PER_HALF
             return None
 
-        def step(i):
-            to_mix = half_closed_by(i - 2)
-            to_transpose = half_closed_by(i - 3)
-            to_quantise = half_closed_by(i - 4)
+        LAST = HALVES - 1
+        for i in range(GROUPS + 1):
+            to_mix, to_transpose, to_quantise = half_closed_by(i - 2), half_closed_by(i - 3), half_closed_by(i - 4)
             if to_transpose is not None:
                 round_mixed(to_transpose)
-            if 0 <= i - 1 < GROUPS:
-                attn_mx[i - 1] = quantise(stage, attn_grouped[i - 1], GROUP_HEADS * QUERIES, "attn")
+            if i >= 1:
+                regroup_v(i - 1)
+                quantise_group(i - 1)
+                quantise_v(i - 1)
             if to_quantise is not None:
-                merged_mx[to_quantise] = quantise(kept, merged_grouped[to_quantise], QUERIES, "merged")
+                quantise_merged(to_quantise)
             if i < GROUPS:
                 transpose_attn(i)
-                regroup_v(i)
             if to_transpose is not None:
                 transpose_merged(to_transpose)
-            if 0 <= i - FIRST_PROJECTION - 1 < WINDOWS:
-                finish_window(i - FIRST_PROJECTION - 1)
-            if i < GROUPS:
-                v_mx[i] = quantise(stage, v_grouped[i], GROUP_HEADS * HEAD_DIM, "v")
             if to_mix is not None:
                 for j in range(to_mix * GROUPS_PER_HALF, (to_mix + 1) * GROUPS_PER_HALF):
                     mix_values(j)
-            if 0 <= i - FIRST_PROJECTION < WINDOWS:
-                project_window(i - FIRST_PROJECTION)
-
-        step(0)
-        spread_bias()
-        for i in range(1, FIRST_PROJECTION + WINDOWS + 1):
-            step(i)
+            if i == 1:
+                spread_bias()
+        for j in range(GROUPS - GROUPS_PER_HALF, GROUPS):
+            mix_values(j)
+        quantise_merged(LAST - 1)
+        round_mixed(LAST)
+        project(0, 0)
+        project(0, 1)
+        transpose_merged(LAST)
+        finish_window(0)
+        quantise_merged(LAST)
+        project(1, 0)
+        project(1, 1)
+        finish_window(1)
+        project(2, 0)
+        project(2, 1)
+        finish_window(2)

@@ -26,10 +26,15 @@ N_TILES = CHANNELS // N_TILE
 GROUP_HEADS = 4
 GROUPS_PER_WINDOW = HEADS // GROUP_HEADS
 GROUPS = WINDOWS * GROUPS_PER_WINDOW
+HEAD_WORDS = HEAD_DIM // PACK
 GROUPS_PER_HALF = K_PASS // (GROUP_HEADS * HEAD_DIM)
 HALVES = WINDOWS * PASSES
 QUERY_RUN = 4
 QUERY_RUNS = QUERIES // QUERY_RUN
+MIX_HEADS = 4
+MIX_COLS = MIX_HEADS * HEAD_DIM
+HEADS_PER_BANK = N_TILE // MIX_COLS
+MIX_BANKS = GROUP_HEADS // HEADS_PER_BANK
 KEY_WORDS = KEYS // 2
 WORD_PLANES = 2
 
@@ -45,9 +50,9 @@ def tile_hieramaskunitattention_pb_kernel(tc, attn, v, proj_w_words, proj_w_scal
         stage = ctx.enter_context(tc.tile_pool(name="stage", bufs=4))
         results = ctx.enter_context(tc.tile_pool(name="results", bufs=WINDOWS * N_TILES))
         kept = ctx.enter_context(tc.tile_pool(name="kept", bufs=HALVES))
-        psum_mixed = ctx.enter_context(tc.psum_pool(name="psum_mixed", bufs=1))
+        psum_mixed = ctx.enter_context(tc.psum_pool(name="psum_mixed", bufs=MIX_BANKS))
         psum_merged = ctx.enter_context(tc.psum_pool(name="psum_merged", bufs=1))
-        psum_turns = ctx.enter_context(tc.psum_pool(name="psum_turns", bufs=WINDOWS * N_TILES))
+        psum_turns = ctx.enter_context(tc.psum_pool(name="psum_turns", bufs=7 - MIX_BANKS))
 
         ident_f32 = const.tile([P, P], F32)
         make_identity(nc, ident_f32[:])
@@ -157,29 +162,38 @@ def tile_hieramaskunitattention_pb_kernel(tc, attn, v, proj_w_words, proj_w_scal
             v_grouped[i] = grouped
 
         def mix_values(i):
-            half, place = i // GROUPS_PER_HALF, i % GROUPS_PER_HALF
-            if place == 0:
-                mixed[half] = psum_mixed.tile([P, K_PASS], F32, name="mixed")
+            mixed[i] = []
+            for k in range(MIX_BANKS):
+                mixed[i].append(psum_mixed.tile([P, N_TILE], F32, tag="mixed", name="mixed"))
             a_codes, a_scales = attn_mx[i]
             v_codes, v_scales = v_mx[i]
             for h in range(GROUP_HEADS):
                 q_cols = slice(h * QUERIES, (h + 1) * QUERIES)
-                d_cols = slice(h * HEAD_DIM, (h + 1) * HEAD_DIM)
-                first = (place * GROUP_HEADS + h) * HEAD_DIM
+                first = h // MIX_HEADS * MIX_COLS
+                v_cols = slice(first, first + MIX_COLS)
+                place = h % HEADS_PER_BANK * MIX_COLS
                 nc.tensor.matmul_mx(
-                    out=mixed[half][:, first : first + HEAD_DIM],
+                    out=mixed[i][h // HEADS_PER_BANK][:, place : place + MIX_COLS],
                     lhsT=a_codes[:, q_cols].bitcast(FP8X4),
                     lhsT_scale=a_scales[:, q_cols],
-                    rhs=v_codes[:, d_cols].bitcast(FP8X4),
-                    rhs_scale=v_scales[:, d_cols],
+                    rhs=v_codes[:, v_cols].bitcast(FP8X4),
+                    rhs_scale=v_scales[:, v_cols],
                     start=True,
                     stop=True,
                 )
 
-        def round_mixed(half):
-            rows = stage.tile([P, PACK, P], BF16, name="merged_rows")
-            nc.scalar.copy(out=rows[:], in_=mixed[half][:].rearrange("p (c t) -> p t c", t=PACK))
-            merged_rows[half] = rows
+        def round_mixed(i):
+            half, place = i // GROUPS_PER_HALF, i % GROUPS_PER_HALF
+            if place == 0:
+                merged_rows[half] = stage.tile([P, PACK, P], BF16, name="merged_rows")
+            rows = merged_rows[half]
+            for k in range(MIX_BANKS):
+                first = (place * GROUP_HEADS + k * HEADS_PER_BANK) * HEAD_WORDS
+                own = mixed[i][k][:].rearrange("p (a j) -> p a j", j=HEAD_DIM)[:, k * HEADS_PER_BANK :: MIX_HEADS + 1, :]
+                nc.scalar.copy(
+                    out=rows[:, :, first : first + HEADS_PER_BANK * HEAD_WORDS].rearrange("p t (a c) -> p t a c", a=HEADS_PER_BANK),
+                    in_=own.rearrange("p a (c t) -> p t a c", t=PACK),
+                )
 
         def transpose_merged(half):
             flipped = psum_merged.tile([P, PACK, P], BF16, name="merged_flipped")
@@ -230,9 +244,9 @@ def tile_hieramaskunitattention_pb_kernel(tc, attn, v, proj_w_words, proj_w_scal
 
         LAST = HALVES - 1
         for i in range(GROUPS + 1):
-            to_mix, to_transpose, to_quantise = half_closed_by(i - 2), half_closed_by(i - 3), half_closed_by(i - 4)
-            if to_transpose is not None:
-                round_mixed(to_transpose)
+            to_transpose, to_quantise = half_closed_by(i - 3), half_closed_by(i - 4)
+            if i >= 3:
+                round_mixed(i - 3)
             if i >= 1:
                 regroup_v(i - 1)
                 quantise_group(i - 1)
@@ -243,15 +257,14 @@ def tile_hieramaskunitattention_pb_kernel(tc, attn, v, proj_w_words, proj_w_scal
                 transpose_attn(i)
             if to_transpose is not None:
                 transpose_merged(to_transpose)
-            if to_mix is not None:
-                for j in range(to_mix * GROUPS_PER_HALF, (to_mix + 1) * GROUPS_PER_HALF):
-                    mix_values(j)
+            if i >= 2:
+                mix_values(i - 2)
             if i == 1:
                 spread_bias()
-        for j in range(GROUPS - GROUPS_PER_HALF, GROUPS):
-            mix_values(j)
+        round_mixed(GROUPS - 2)
+        mix_values(GROUPS - 1)
         quantise_merged(LAST - 1)
-        round_mixed(LAST)
+        round_mixed(GROUPS - 1)
         project(0, 0)
         project(0, 1)
         transpose_merged(LAST)

@@ -50,14 +50,11 @@ def tile_hieramaskunitattention_pb_kernel(tc, attn, v, proj_w_words, proj_w_scal
         stage = ctx.enter_context(tc.tile_pool(name="stage", bufs=4))
         results = ctx.enter_context(tc.tile_pool(name="results", bufs=WINDOWS * N_TILES))
         kept = ctx.enter_context(tc.tile_pool(name="kept", bufs=HALVES))
-        psum_mixed = ctx.enter_context(tc.psum_pool(name="psum_mixed", bufs=MIX_BANKS))
         psum_merged = ctx.enter_context(tc.psum_pool(name="psum_merged", bufs=1))
-        psum_turns = ctx.enter_context(tc.psum_pool(name="psum_turns", bufs=7 - MIX_BANKS))
+        psum_turns = ctx.enter_context(tc.psum_pool(name="psum_turns", bufs=7))
 
         ident_f32 = const.tile([P, P], F32)
         make_identity(nc, ident_f32[:])
-        ident_bf16 = const.tile([P, P], BF16)
-        make_identity(nc, ident_bf16[:])
 
         w_scales = const.tile([P, PASSES, CHANNELS], U8, align_bytes=64)
         nc.vector.memset(w_scales[:].bitcast(I32), 0)
@@ -67,45 +64,57 @@ def tile_hieramaskunitattention_pb_kernel(tc, attn, v, proj_w_words, proj_w_scal
         ones = const.tile([P, P], BF16)
         nc.vector.memset(ones[:], 1.0)
 
-        attn_rows = []
-        v_rows = []
+        attn_rows = {}
+        v_rows = {}
         w_words = const.tile([P, PASSES, CHANNELS * PACK], U8, align_bytes=64)
 
         def window_and_heads(i):
             first_head = GROUP_HEADS * (i % GROUPS_PER_WINDOW)
             return i // GROUPS_PER_WINDOW, slice(first_head, first_head + GROUP_HEADS)
 
-        def load_attn(i):
-            w, heads = window_and_heads(i)
-            attn_in = loads.tile([P, QUERY_RUN * KEYS], BF16, name="attn_in")
+        def load_attn(i, heads=GROUP_HEADS, first=0):
+            w, group = window_and_heads(i)
+            start = group.start + first
+            attn_in = loads.tile([P, heads * KEYS], BF16, name="attn_in%d" % heads)
             nc.sync.dma_start(
                 out=attn_in[:],
-                in_=attn[0, heads, w].rearrange("h (r j) k -> r h (j k)", j=QUERY_RUN),
+                in_=attn[0, start : start + heads, w].rearrange("h (r j) k -> r h (j k)", j=heads),
             )
-            attn_rows.append(attn_in)
+            attn_rows[i, first] = attn_in
 
         def load_v(i):
             w, heads = window_and_heads(i)
             v_in = loads.tile([P, GROUP_HEADS, PACK * HEAD_DIM], BF16, name="v_in")
             nc.sync.dma_start(out=v_in[:], in_=v[0, heads, w].rearrange("h (p t) d -> p h (t d)", t=PACK))
-            v_rows.append(v_in)
+            v_rows[i] = v_in
 
-        for i in range(GROUPS):
+        def load_small():
+            for quadrant in range(4):
+                nc.sync.dma_start(
+                    out=w_scales[32 * quadrant : 32 * quadrant + 4].bitcast(I32),
+                    in_=proj_w_scales[:, 4 * quadrant : 4 * quadrant + 4, :].rearrange("g r n -> r g n").bitcast(I32),
+                )
+            nc.sync.dma_start(out=bias_rows[0:1, :], in_=proj_b.unsqueeze(0))
+
+        def load_weight(n=None):
+            a, b = (0, CHANNELS) if n is None else (n * N_TILE, (n + 1) * N_TILE)
+            nc.sync.dma_start(
+                out=w_words[:, :, a * PACK : b * PACK].bitcast(I32),
+                in_=proj_w_words[:, :, a:b].rearrange("g p n t -> p g (n t)").bitcast(I32),
+            )
+
+        for i in range(GROUPS - 1):
             load_attn(i)
             if i > 0:
                 load_v(i - 1)
             if i == 0:
-                for quadrant in range(4):
-                    nc.sync.dma_start(
-                        out=w_scales[32 * quadrant : 32 * quadrant + 4].bitcast(I32),
-                        in_=proj_w_scales[:, 4 * quadrant : 4 * quadrant + 4, :].rearrange("g r n -> r g n").bitcast(I32),
-                    )
-                nc.sync.dma_start(out=bias_rows[0:1, :], in_=proj_b.unsqueeze(0))
+                load_small()
+        load_v(GROUPS - 2)
+        load_attn(GROUPS - 1, 2, 0)
+        load_attn(GROUPS - 1, 2, 2)
         load_v(GROUPS - 1)
-        nc.sync.dma_start(
-            out=w_words[:].bitcast(I32),
-            in_=proj_w_words.rearrange("g p n t -> p g (n t)").bitcast(I32),
-        )
+        load_weight(0)
+        load_weight(1)
 
         bias_all = const.tile([P, CHANNELS], BF16)
 
@@ -128,30 +137,50 @@ def tile_hieramaskunitattention_pb_kernel(tc, attn, v, proj_w_words, proj_w_scal
         merged_mx = {}
         out_banks = {}
 
-        def transpose_attn(i):
-            words = attn_rows[i][:].bitcast(F32)
-            grouped = stage.tile([P, GROUP_HEADS * QUERIES * PACK], BF16, align_bytes=64, name="attn_grouped")
-            grouped_words = grouped[:].bitcast(F32).rearrange(
-                "p (h r b ju) -> p b h r ju", h=GROUP_HEADS, r=QUERY_RUNS, b=2
+        def transpose_attn(i, heads=GROUP_HEADS, first=0):
+            words = attn_rows[i, first][:].bitcast(F32)
+            if first == 0:
+                attn_grouped[i] = stage.tile([P, GROUP_HEADS * QUERIES * PACK], BF16, align_bytes=64, name="attn_grouped")
+            width = QUERIES * PACK
+            grouped_words = attn_grouped[i][:, first * width : (first + heads) * width].bitcast(F32).rearrange(
+                "p (h r b ju) -> p b h r ju", h=heads, r=QUERIES // heads, b=heads // 2
             )
-            for b in range(2):
+            for b in range(heads // 2):
                 flipped = psum_turns.tile([P, 2, WORD_PLANES, P], F32, tag="turn")
                 for j in range(2):
-                    first = (2 * b + j) * KEY_WORDS
+                    start = (2 * b + j) * KEY_WORDS
                     for u in range(WORD_PLANES):
                         nc.tensor.transpose(
-                            flipped[:, j, u, :], words[:, first + u : first + KEY_WORDS : WORD_PLANES], ident_f32[:]
+                            flipped[:, j, u, :], words[:, start + u : start + KEY_WORDS : WORD_PLANES], ident_f32[:]
                         )
                 nc.scalar.copy(
-                    out=grouped_words[:, b], in_=flipped[:].rearrange("p j u (r h) -> p h r (j u)", h=GROUP_HEADS)
+                    out=grouped_words[:, b], in_=flipped[:].rearrange("p j u (r h) -> p h r (j u)", h=heads)
                 )
-            attn_grouped[i] = grouped
 
-        def quantise(pool, grouped, width, name):
+        def quantise_into(pair, grouped, first, width):
+            codes, scales = pair
+            cols = slice(first, first + width)
+            nc.vector.quantize_mx(
+                out=codes[:, cols].bitcast(FP8X4), scales=scales[:, cols], in_=grouped[:, first * PACK : (first + width) * PACK]
+            )
+
+        def mx_pair(pool, width, name):
             codes = pool.tile([P, width], U32, align_bytes=64, name=name + "_codes")
             scales = pool.tile([P, width], U8, align_bytes=64, name=name + "_scales")
-            nc.vector.quantize_mx(out=codes[:].bitcast(FP8X4), scales=scales[:], in_=grouped[:])
             return codes, scales
+
+        def quantise_attn(i, heads=GROUP_HEADS, first=0):
+            if first == 0:
+                attn_mx[i] = mx_pair(stage, GROUP_HEADS * QUERIES, "attn")
+            quantise_into(attn_mx[i], attn_grouped[i], first * QUERIES, heads * QUERIES)
+
+        def quantise_v(i):
+            v_mx[i] = mx_pair(stage, GROUP_HEADS * HEAD_DIM, "v")
+            quantise_into(v_mx[i], v_grouped[i], 0, GROUP_HEADS * HEAD_DIM)
+
+        def quantise_merged(half):
+            merged_mx[half] = mx_pair(kept, QUERIES, "merged")
+            quantise_into(merged_mx[half], merged_grouped[half], 0, QUERIES)
 
         def regroup_v(i):
             grouped = stage.tile([P, GROUP_HEADS * HEAD_DIM * PACK], BF16, align_bytes=64, name="v_grouped")
@@ -161,13 +190,14 @@ def tile_hieramaskunitattention_pb_kernel(tc, attn, v, proj_w_words, proj_w_scal
             )
             v_grouped[i] = grouped
 
-        def mix_values(i):
-            mixed[i] = []
-            for k in range(MIX_BANKS):
-                mixed[i].append(psum_mixed.tile([P, N_TILE], F32, tag="mixed", name="mixed"))
+        def mix_values(i, heads=GROUP_HEADS, first_head=0):
+            if first_head == 0:
+                mixed[i] = []
+                for k in range(MIX_BANKS):
+                    mixed[i].append(psum_turns.tile([P, N_TILE], F32, tag="turn", name="mixed"))
             a_codes, a_scales = attn_mx[i]
             v_codes, v_scales = v_mx[i]
-            for h in range(GROUP_HEADS):
+            for h in range(first_head, first_head + heads):
                 q_cols = slice(h * QUERIES, (h + 1) * QUERIES)
                 first = h // MIX_HEADS * MIX_COLS
                 v_cols = slice(first, first + MIX_COLS)
@@ -182,35 +212,37 @@ def tile_hieramaskunitattention_pb_kernel(tc, attn, v, proj_w_words, proj_w_scal
                     stop=True,
                 )
 
-        def round_mixed(i):
+        def round_mixed(i, banks=(0, 1)):
             half, place = i // GROUPS_PER_HALF, i % GROUPS_PER_HALF
-            if place == 0:
-                merged_rows[half] = stage.tile([P, PACK, P], BF16, name="merged_rows")
+            if place == 0 and 0 in banks:
+                merged_rows[half] = stage.tile([P, K_PASS], BF16, name="merged_rows")
             rows = merged_rows[half]
-            for k in range(MIX_BANKS):
+            for k in banks:
                 first = (place * GROUP_HEADS + k * HEADS_PER_BANK) * HEAD_WORDS
                 own = mixed[i][k][:].rearrange("p (a j) -> p a j", j=HEAD_DIM)[:, k * HEADS_PER_BANK :: MIX_HEADS + 1, :]
                 nc.scalar.copy(
-                    out=rows[:, :, first : first + HEADS_PER_BANK * HEAD_WORDS].rearrange("p t (a c) -> p t a c", a=HEADS_PER_BANK),
-                    in_=own.rearrange("p a (c t) -> p t a c", t=PACK),
+                    out=rows[:].rearrange("p (u c e) -> p u c e", u=WORD_PLANES, e=2)[:, :, first : first + HEADS_PER_BANK * HEAD_WORDS, :].rearrange("p u (a c) e -> p a u c e", a=HEADS_PER_BANK),
+                    in_=own.rearrange("p a (c u e) -> p a u c e", u=WORD_PLANES, e=2),
                 )
 
         def transpose_merged(half):
-            flipped = psum_merged.tile([P, PACK, P], BF16, name="merged_flipped")
-            for t in range(PACK):
-                nc.tensor.transpose(flipped[:, t, :], merged_rows[half][:, t, :], ident_bf16[:])
+            words = merged_rows[half][:].bitcast(F32)
+            flipped = psum_merged.tile([P, WORD_PLANES, P], F32, name="merged_flipped")
+            for u in range(WORD_PLANES):
+                nc.tensor.transpose(flipped[:, u, :], words[:, u * P : (u + 1) * P], ident_f32[:])
             grouped = stage.tile([P, QUERIES * PACK], BF16, align_bytes=64, name="merged_grouped")
             nc.scalar.copy(
-                out=grouped[:].rearrange("p (q t) -> p q t", t=PACK), in_=flipped[:].rearrange("p t q -> p q t")
+                out=grouped[:].bitcast(F32).rearrange("p (q u) -> p q u", u=WORD_PLANES),
+                in_=flipped[:].rearrange("p u q -> p q u"),
             )
             merged_grouped[half] = grouped
 
-        def project(w, g):
+        def project(w, g, tiles=range(N_TILES)):
             if g == 0:
-                for n in range(N_TILES):
+                for n in tiles:
                     out_banks[w, n] = psum_turns.tile([P, N_TILE], F32, tag="turn", name="out_bank")
             m_codes, m_scales = merged_mx[w * PASSES + g]
-            for n in range(N_TILES):
+            for n in tiles:
                 nc.tensor.matmul_mx(
                     out=out_banks[w, n][:],
                     lhsT=m_codes[:].bitcast(FP8X4),
@@ -221,21 +253,12 @@ def tile_hieramaskunitattention_pb_kernel(tc, attn, v, proj_w_words, proj_w_scal
                     stop=(g == PASSES - 1),
                 )
 
-        def finish_window(w):
-            for n in range(N_TILES):
+        def finish_window(w, tiles=range(N_TILES)):
+            for n in tiles:
                 cols = slice(n * N_TILE, (n + 1) * N_TILE)
                 result = results.tile([P, N_TILE], F32)
                 nc.vector.tensor_add(out=result[:], in0=out_banks[w, n][:], in1=bias_all[:, cols])
                 nc.sync.dma_start(out=out_rows[w][:, cols], in_=result[:])
-
-        def quantise_group(i):
-            attn_mx[i] = quantise(stage, attn_grouped[i], GROUP_HEADS * QUERIES, "attn")
-
-        def quantise_v(i):
-            v_mx[i] = quantise(stage, v_grouped[i], GROUP_HEADS * HEAD_DIM, "v")
-
-        def quantise_merged(half):
-            merged_mx[half] = quantise(kept, merged_grouped[half], QUERIES, "merged")
 
         def half_closed_by(j):
             if 0 <= j < GROUPS and j % GROUPS_PER_HALF == GROUPS_PER_HALF - 1:
@@ -243,36 +266,56 @@ def tile_hieramaskunitattention_pb_kernel(tc, attn, v, proj_w_words, proj_w_scal
             return None
 
         LAST = HALVES - 1
-        for i in range(GROUPS + 1):
+        for i in range(GROUPS - 1):
             to_transpose, to_quantise = half_closed_by(i - 3), half_closed_by(i - 4)
             if i >= 3:
                 round_mixed(i - 3)
             if i >= 1:
                 regroup_v(i - 1)
-                quantise_group(i - 1)
+                quantise_attn(i - 1)
                 quantise_v(i - 1)
             if to_quantise is not None:
                 quantise_merged(to_quantise)
-            if i < GROUPS:
-                transpose_attn(i)
+            transpose_attn(i)
             if to_transpose is not None:
                 transpose_merged(to_transpose)
             if i >= 2:
                 mix_values(i - 2)
             if i == 1:
                 spread_bias()
-        round_mixed(GROUPS - 2)
-        mix_values(GROUPS - 1)
-        quantise_merged(LAST - 1)
-        round_mixed(GROUPS - 1)
-        project(0, 0)
-        project(0, 1)
+        regroup_v(10)
+        quantise_attn(10)
+        quantise_v(10)
+        round_mixed(8)
+        transpose_attn(11, 2, 0)
+        transpose_attn(11, 2, 2)
+        mix_values(9)
+        round_mixed(9)
+        mix_values(10)
+        quantise_attn(11, 2, 0)
+        regroup_v(11)
+        quantise_attn(11, 2, 2)
+        quantise_v(11)
+        quantise_merged(3)
+        transpose_merged(4)
+        round_mixed(10)
+        quantise_merged(4)
+        project(0, 0, [0])
+        project(0, 1, [0])
+        mix_values(11)
+        finish_window(0, [0])
+        round_mixed(11)
+        project(1, 0, [0])
+        project(1, 1, [0])
+        finish_window(1, [0])
         transpose_merged(LAST)
-        finish_window(0)
+        project(0, 0, [1])
+        project(0, 1, [1])
         quantise_merged(LAST)
-        project(1, 0)
-        project(1, 1)
-        finish_window(1)
+        finish_window(0, [1])
+        project(1, 0, [1])
+        project(1, 1, [1])
+        finish_window(1, [1])
         project(2, 0)
         project(2, 1)
         finish_window(2)

@@ -31,10 +31,9 @@ GROUPS_PER_HALF = K_PASS // (GROUP_HEADS * HEAD_DIM)
 HALVES = WINDOWS * PASSES
 QUERY_RUN = 4
 QUERY_RUNS = QUERIES // QUERY_RUN
-MIX_HEADS = 4
-MIX_COLS = MIX_HEADS * HEAD_DIM
-HEADS_PER_BANK = N_TILE // MIX_COLS
-MIX_BANKS = GROUP_HEADS // HEADS_PER_BANK
+SPANS = (4, 4)
+BANK_HEADS = len(SPANS)
+RUN = 4
 KEY_WORDS = KEYS // 2
 WORD_PLANES = 2
 
@@ -88,13 +87,15 @@ def tile_hieramaskunitattention_pb_kernel(tc, attn, v, proj_w_words, proj_w_scal
             nc.sync.dma_start(out=v_in[:], in_=v[0, heads, w].rearrange("h (p t) d -> p h (t d)", t=PACK))
             v_rows[i] = v_in
 
-        def load_small():
+        def load_bias():
+            nc.sync.dma_start(out=bias_rows[0:1, :], in_=proj_b.unsqueeze(0))
+
+        def load_scales():
             for quadrant in range(4):
                 nc.sync.dma_start(
                     out=w_scales[32 * quadrant : 32 * quadrant + 4].bitcast(I32),
                     in_=proj_w_scales[:, 4 * quadrant : 4 * quadrant + 4, :].rearrange("g r n -> r g n").bitcast(I32),
                 )
-            nc.sync.dma_start(out=bias_rows[0:1, :], in_=proj_b.unsqueeze(0))
 
         def load_weight(n=None):
             a, b = (0, CHANNELS) if n is None else (n * N_TILE, (n + 1) * N_TILE)
@@ -108,11 +109,12 @@ def tile_hieramaskunitattention_pb_kernel(tc, attn, v, proj_w_words, proj_w_scal
             if i > 0:
                 load_v(i - 1)
             if i == 0:
-                load_small()
+                load_bias()
         load_v(GROUPS - 2)
         load_attn(GROUPS - 1, 2, 0)
         load_attn(GROUPS - 1, 2, 2)
         load_v(GROUPS - 1)
+        load_scales()
         load_weight(0)
         load_weight(1)
 
@@ -185,25 +187,29 @@ def tile_hieramaskunitattention_pb_kernel(tc, attn, v, proj_w_words, proj_w_scal
         def regroup_v(i):
             grouped = stage.tile([P, GROUP_HEADS * HEAD_DIM * PACK], BF16, align_bytes=64, name="v_grouped")
             nc.vector.tensor_copy(
-                out=grouped[:].rearrange("p (h d t) -> p h d t", h=GROUP_HEADS, t=PACK),
-                in_=v_rows[i][:].rearrange("p h (t d) -> p h d t", t=PACK),
+                out=grouped[:].rearrange("p (h c i t) -> p h c t i", h=GROUP_HEADS, i=RUN, t=PACK),
+                in_=v_rows[i][:].rearrange("p h (t c i) -> p h c t i", t=PACK, i=RUN),
             )
             v_grouped[i] = grouped
 
-        def mix_values(i, heads=GROUP_HEADS, first_head=0):
-            if first_head == 0:
-                mixed[i] = []
-                for k in range(MIX_BANKS):
-                    mixed[i].append(psum_turns.tile([P, N_TILE], F32, tag="turn", name="mixed"))
+        def mix_values(i):
             a_codes, a_scales = attn_mx[i]
             v_codes, v_scales = v_mx[i]
-            for h in range(first_head, first_head + heads):
+            mixed[i] = []
+            for h in range(GROUP_HEADS):
+                span = SPANS[h % BANK_HEADS]
+                if h % BANK_HEADS == 0:
+                    bank = psum_turns.tile([P, N_TILE], F32, tag="turn", name="mixed")
+                    own = []
+                    mixed[i].append((bank, own))
+                    place = 0
+                first = h // span * span
+                own.append(place // HEAD_DIM + h - first)
+                cols = span * HEAD_DIM
                 q_cols = slice(h * QUERIES, (h + 1) * QUERIES)
-                first = h // MIX_HEADS * MIX_COLS
-                v_cols = slice(first, first + MIX_COLS)
-                place = h % HEADS_PER_BANK * MIX_COLS
+                v_cols = slice(first * HEAD_DIM, first * HEAD_DIM + cols)
                 nc.tensor.matmul_mx(
-                    out=mixed[i][h // HEADS_PER_BANK][:, place : place + MIX_COLS],
+                    out=bank[:, place : place + cols],
                     lhsT=a_codes[:, q_cols].bitcast(FP8X4),
                     lhsT_scale=a_scales[:, q_cols],
                     rhs=v_codes[:, v_cols].bitcast(FP8X4),
@@ -211,18 +217,18 @@ def tile_hieramaskunitattention_pb_kernel(tc, attn, v, proj_w_words, proj_w_scal
                     start=True,
                     stop=True,
                 )
+                place += cols
 
-        def round_mixed(i, banks=(0, 1)):
+        def round_mixed(i):
             half, place = i // GROUPS_PER_HALF, i % GROUPS_PER_HALF
-            if place == 0 and 0 in banks:
+            if place == 0:
                 merged_rows[half] = stage.tile([P, K_PASS], BF16, name="merged_rows")
-            rows = merged_rows[half]
-            for k in banks:
-                first = (place * GROUP_HEADS + k * HEADS_PER_BANK) * HEAD_WORDS
-                own = mixed[i][k][:].rearrange("p (a j) -> p a j", j=HEAD_DIM)[:, k * HEADS_PER_BANK :: MIX_HEADS + 1, :]
+            rows = merged_rows[half][:].rearrange("p (u c e) -> p u c e", u=WORD_PLANES, e=2)
+            for k, (bank, (a, b)) in enumerate(mixed[i]):
+                first = (place * GROUP_HEADS + k * BANK_HEADS) * HEAD_WORDS
                 nc.scalar.copy(
-                    out=rows[:].rearrange("p (u c e) -> p u c e", u=WORD_PLANES, e=2)[:, :, first : first + HEADS_PER_BANK * HEAD_WORDS, :].rearrange("p u (a c) e -> p a u c e", a=HEADS_PER_BANK),
-                    in_=own.rearrange("p a (c u e) -> p a u c e", u=WORD_PLANES, e=2),
+                    out=rows[:, :, first : first + BANK_HEADS * HEAD_WORDS, :].rearrange("p u (a c) e -> p a u c e", a=BANK_HEADS),
+                    in_=bank[:].rearrange("p (a c u e) -> p a u c e", c=HEAD_WORDS, u=WORD_PLANES, e=2)[:, a : b + 1 : b - a],
                 )
 
         def transpose_merged(half):
@@ -237,28 +243,29 @@ def tile_hieramaskunitattention_pb_kernel(tc, attn, v, proj_w_words, proj_w_scal
             )
             merged_grouped[half] = grouped
 
-        def project(w, g, tiles=range(N_TILES)):
-            if g == 0:
-                for n in tiles:
-                    out_banks[w, n] = psum_turns.tile([P, N_TILE], F32, tag="turn", name="out_bank")
+        def project(w, g, tiles):
             m_codes, m_scales = merged_mx[w * PASSES + g]
-            for n in tiles:
+            for first, width in tiles:
+                if g == 0:
+                    out_banks[w, first] = psum_turns.tile([P, N_TILE], F32, tag="turn", name="out_bank")
                 nc.tensor.matmul_mx(
-                    out=out_banks[w, n][:],
+                    out=out_banks[w, first][:, :width],
                     lhsT=m_codes[:].bitcast(FP8X4),
                     lhsT_scale=m_scales[:],
-                    rhs=w_words[:, g, n * N_TILE * PACK : (n + 1) * N_TILE * PACK].bitcast(FP8X4),
-                    rhs_scale=w_scales[:, g, n * N_TILE : (n + 1) * N_TILE],
+                    rhs=w_words[:, g, first * PACK : (first + width) * PACK].bitcast(FP8X4),
+                    rhs_scale=w_scales[:, g, first : first + width],
                     start=(g == 0),
                     stop=(g == PASSES - 1),
                 )
 
-        def finish_window(w, tiles=range(N_TILES)):
-            for n in tiles:
-                cols = slice(n * N_TILE, (n + 1) * N_TILE)
+        def finish(w, tiles):
+            for first, width in tiles:
+                cols = slice(first, first + width)
                 result = results.tile([P, N_TILE], F32)
-                nc.vector.tensor_add(out=result[:], in0=out_banks[w, n][:], in1=bias_all[:, cols])
-                nc.sync.dma_start(out=out_rows[w][:, cols], in_=result[:])
+                nc.vector.tensor_add(out=result[:, :width], in0=out_banks[w, first][:, :width], in1=bias_all[:, cols])
+                nc.sync.dma_start(out=out_rows[w][:, cols], in_=result[:, :width])
+
+        LEFT, RIGHT = [(0, N_TILE)], [(N_TILE, N_TILE)]
 
         def half_closed_by(j):
             if 0 <= j < GROUPS and j % GROUPS_PER_HALF == GROUPS_PER_HALF - 1:
@@ -300,22 +307,22 @@ def tile_hieramaskunitattention_pb_kernel(tc, attn, v, proj_w_words, proj_w_scal
         transpose_merged(4)
         round_mixed(10)
         quantise_merged(4)
-        project(0, 0, [0])
-        project(0, 1, [0])
+        project(0, 0, LEFT)
+        project(0, 1, LEFT)
         mix_values(11)
-        finish_window(0, [0])
+        finish(0, LEFT)
         round_mixed(11)
-        project(1, 0, [0])
-        project(1, 1, [0])
-        finish_window(1, [0])
+        project(1, 0, LEFT)
+        project(1, 1, LEFT)
+        finish(1, LEFT)
         transpose_merged(LAST)
-        project(0, 0, [1])
-        project(0, 1, [1])
+        project(0, 0, RIGHT)
+        project(0, 1, RIGHT)
         quantise_merged(LAST)
-        finish_window(0, [1])
-        project(1, 0, [1])
-        project(1, 1, [1])
-        finish_window(1, [1])
-        project(2, 0)
-        project(2, 1)
-        finish_window(2)
+        finish(0, RIGHT)
+        project(1, 0, RIGHT)
+        project(1, 1, RIGHT)
+        finish(1, RIGHT)
+        project(2, 0, LEFT + RIGHT)
+        project(2, 1, LEFT + RIGHT)
+        finish(2, LEFT + RIGHT)

from contextlib import ExitStack

import concourse.mybir as mybir
from concourse.masks import make_identity

BF16 = mybir.dt.bfloat16
F32 = mybir.dt.float32
I32 = mybir.dt.int32
U32 = mybir.dt.uint32
U8 = mybir.dt.uint8
FP8X4 = mybir.dt.float8_e4m3fn_x4

P = 128
PACK = 4
HEADS = 16
WINDOWS = 3
QUERIES = 128
KEYS = 512
HEAD_DIM = 64
CHANNELS = HEADS * HEAD_DIM
K_PASS = P * PACK
PASSES = CHANNELS // K_PASS
N_TILE = 512
N_TILES = CHANNELS // N_TILE

GROUP_HEADS = 4
GROUPS_PER_WINDOW = HEADS // GROUP_HEADS
GROUPS = WINDOWS * GROUPS_PER_WINDOW
HEAD_WORDS = HEAD_DIM // PACK
GROUPS_PER_HALF = K_PASS // (GROUP_HEADS * HEAD_DIM)
HALVES = WINDOWS * PASSES
QUERY_RUN = 4
QUERY_RUNS = QUERIES // QUERY_RUN
SPANS = (4, 4)
BANK_HEADS = len(SPANS)
RUN = 4
KEY_WORDS = KEYS // 2
WORD_PLANES = 2

FLOPS = 2 * HEADS * WINDOWS * QUERIES * KEYS * HEAD_DIM + 2 * WINDOWS * QUERIES * CHANNELS * CHANNELS


def tile_hieramaskunitattention_pb_kernel(tc, attn, v, proj_w_words, proj_w_scales, proj_b, out):
    nc = tc.nc
    with ExitStack() as ctx:
        ctx.enter_context(tc.manual_schedule())
        const = ctx.enter_context(tc.tile_pool(name="const", bufs=1))
        loads = ctx.enter_context(tc.tile_pool(name="loads", bufs=GROUPS))
        stage = ctx.enter_context(tc.tile_pool(name="stage", bufs=4))
        results = ctx.enter_context(tc.tile_pool(name="results", bufs=WINDOWS * N_TILES))
        kept = ctx.enter_context(tc.tile_pool(name="kept", bufs=HALVES))
        psum_merged = ctx.enter_context(tc.psum_pool(name="psum_merged", bufs=1))
        psum_turns = ctx.enter_context(tc.psum_pool(name="psum_turns", bufs=7))

        ident_f32 = const.tile([P, P], F32)
        make_identity(nc, ident_f32[:])

        w_scales = const.tile([P, PASSES, CHANNELS], U8, align_bytes=64)
        nc.vector.memset(w_scales[:].bitcast(I32), 0)

        bias_rows = const.tile([P, CHANNELS], BF16)
        nc.vector.memset(bias_rows[:], 0.0)
        ones = const.tile([P, P], BF16)
        nc.vector.memset(ones[:], 1.0)

        attn_rows = {}
        v_rows = {}
        w_words = const.tile([P, PASSES, CHANNELS * PACK], U8, align_bytes=64)

        def window_and_heads(i):
            first_head = GROUP_HEADS * (i % GROUPS_PER_WINDOW)
            return i // GROUPS_PER_WINDOW, slice(first_head, first_head + GROUP_HEADS)

        def load_attn(i, heads=GROUP_HEADS, first=0):
            w, group = window_and_heads(i)
            start = group.start + first
            attn_in = loads.tile([P, heads * KEYS], BF16, name="attn_in%d" % heads)
            nc.sync.dma_start(
                out=attn_in[:],
                in_=attn[0, start : start + heads, w].rearrange("h (r j) k -> r h (j k)", j=heads),
            )
            attn_rows[i, first] = attn_in

        def load_v(i):
            w, heads = window_and_heads(i)
            v_in = loads.tile([P, GROUP_HEADS, PACK * HEAD_DIM], BF16, name="v_in")
            nc.sync.dma_start(out=v_in[:], in_=v[0, heads, w].rearrange("h (p t) d -> p h (t d)", t=PACK))
            v_rows[i] = v_in

        def load_bias():
            nc.sync.dma_start(out=bias_rows[0:1, :], in_=proj_b.unsqueeze(0))

        def load_scales():
            for quadrant in range(4):
                nc.sync.dma_start(
                    out=w_scales[32 * quadrant : 32 * quadrant + 4].bitcast(I32),
                    in_=proj_w_scales[:, 4 * quadrant : 4 * quadrant + 4, :].rearrange("g r n -> r g n").bitcast(I32),
                )

        def load_weight(n=None):
            a, b = (0, CHANNELS) if n is None else (n * N_TILE, (n + 1) * N_TILE)
            nc.sync.dma_start(
                out=w_words[:, :, a * PACK : b * PACK].bitcast(I32),
                in_=proj_w_words[:, :, a:b].rearrange("g p n t -> p g (n t)").bitcast(I32),
            )

        for i in range(GROUPS - 1):
            load_attn(i)
            if i > 0:
                load_v(i - 1)
            if i == 0:
                load_bias()
        load_v(GROUPS - 2)
        load_attn(GROUPS - 1, 2, 0)
        load_attn(GROUPS - 1, 2, 2)
        load_v(GROUPS - 1)
        load_scales()
        load_weight(0)
        load_weight(1)

        bias_all = const.tile([P, CHANNELS], BF16)

        def spread_bias():
            spread = psum_turns.tile([P, CHANNELS], BF16, tag="turn", name="spread")
            for n in range(N_TILES):
                cols = slice(n * N_TILE, (n + 1) * N_TILE)
                nc.tensor.matmul(out=spread[:, cols], lhsT=ones[:], rhs=bias_rows[:, cols], start=True, stop=True)
            nc.vector.tensor_copy(out=bias_all[:], in_=spread[:])

        out_rows = out[0].rearrange("(q w) n -> w q n", w=WINDOWS)

        attn_grouped = {}
        attn_mx = {}
        v_grouped = {}
        v_mx = {}
        mixed = {}
        merged_rows = {}
        merged_grouped = {}
        merged_mx = {}
        out_banks = {}

        def transpose_attn(i, heads=GROUP_HEADS, first=0):
            words = attn_rows[i, first][:].bitcast(F32)
            if first == 0:
                attn_grouped[i] = stage.tile([P, GROUP_HEADS * QUERIES * PACK], BF16, align_bytes=64, name="attn_grouped")
            width = QUERIES * PACK
            grouped_words = attn_grouped[i][:, first * width : (first + heads) * width].bitcast(F32).rearrange(
                "p (h r b ju) -> p b h r ju", h=heads, r=QUERIES // heads, b=heads // 2
            )
            for b in range(heads // 2):
                flipped = psum_turns.tile([P, 2, WORD_PLANES, P], F32, tag="turn")
                for j in range(2):
                    start = (2 * b + j) * KEY_WORDS
                    for u in range(WORD_PLANES):
                        nc.tensor.transpose(
                            flipped[:, j, u, :], words[:, start + u : start + KEY_WORDS : WORD_PLANES], ident_f32[:]
                        )
                nc.scalar.copy(
                    out=grouped_words[:, b], in_=flipped[:].rearrange("p j u (r h) -> p h r (j u)", h=heads)
                )

        def quantise_into(pair, grouped, first, width):
            codes, scales = pair
            cols = slice(first, first + width)
            nc.vector.quantize_mx(
                out=codes[:, cols].bitcast(FP8X4), scales=scales[:, cols], in_=grouped[:, first * PACK : (first + width) * PACK]
            )

        def mx_pair(pool, width, name):
            codes = pool.tile([P, width], U32, align_bytes=64, name=name + "_codes")
            scales = pool.tile([P, width], U8, align_bytes=64, name=name + "_scales")
            return codes, scales

        def quantise_attn(i, heads=GROUP_HEADS, first=0):
            if first == 0:
                attn_mx[i] = mx_pair(stage, GROUP_HEADS * QUERIES, "attn")
            quantise_into(attn_mx[i], attn_grouped[i], first * QUERIES, heads * QUERIES)

        def quantise_v(i):
            v_mx[i] = mx_pair(stage, GROUP_HEADS * HEAD_DIM, "v")
            quantise_into(v_mx[i], v_grouped[i], 0, GROUP_HEADS * HEAD_DIM)

        def quantise_merged(half):
            merged_mx[half] = mx_pair(kept, QUERIES, "merged")
            quantise_into(merged_mx[half], merged_grouped[half], 0, QUERIES)

        def regroup_v(i):
            grouped = stage.tile([P, GROUP_HEADS * HEAD_DIM * PACK], BF16, align_bytes=64, name="v_grouped")
            nc.vector.tensor_copy(
                out=grouped[:].rearrange("p (h c i t) -> p h c t i", h=GROUP_HEADS, i=RUN, t=PACK),
                in_=v_rows[i][:].rearrange("p h (t c i) -> p h c t i", t=PACK, i=RUN),
            )
            v_grouped[i] = grouped

        def mix_values(i):
            a_codes, a_scales = attn_mx[i]
            v_codes, v_scales = v_mx[i]
            mixed[i] = []
            for h in range(GROUP_HEADS):
                span = SPANS[h % BANK_HEADS]
                if h % BANK_HEADS == 0:
                    bank = psum_turns.tile([P, N_TILE], F32, tag="turn", name="mixed")
                    own = []
                    mixed[i].append((bank, own))
                    place = 0
                first = h // span * span
                own.append(place // HEAD_DIM + h - first)
                cols = span * HEAD_DIM
                q_cols = slice(h * QUERIES, (h + 1) * QUERIES)
                v_cols = slice(first * HEAD_DIM, first * HEAD_DIM + cols)
                nc.tensor.matmul_mx(
                    out=bank[:, place : place + cols],
                    lhsT=a_codes[:, q_cols].bitcast(FP8X4),
                    lhsT_scale=a_scales[:, q_cols],
                    rhs=v_codes[:, v_cols].bitcast(FP8X4),
                    rhs_scale=v_scales[:, v_cols],
                    start=True,
                    stop=True,
                )
                place += cols

        def round_mixed(i):
            half, place = i // GROUPS_PER_HALF, i % GROUPS_PER_HALF
            if place == 0:
                merged_rows[half] = stage.tile([P, K_PASS], BF16, name="merged_rows")
            rows = merged_rows[half][:].rearrange("p (u c e) -> p u c e", u=WORD_PLANES, e=2)
            for k, (bank, (a, b)) in enumerate(mixed[i]):
                first = (place * GROUP_HEADS + k * BANK_HEADS) * HEAD_WORDS
                nc.scalar.copy(
                    out=rows[:, :, first : first + BANK_HEADS * HEAD_WORDS, :].rearrange("p u (a c) e -> p a u c e", a=BANK_HEADS),
                    in_=bank[:].rearrange("p (a c u e) -> p a u c e", c=HEAD_WORDS, u=WORD_PLANES, e=2)[:, a : b + 1 : b - a],
                )

        def transpose_merged(half):
            words = merged_rows[half][:].bitcast(F32)
            flipped = psum_merged.tile([P, WORD_PLANES, P], F32, name="merged_flipped")
            for u in range(WORD_PLANES):
                nc.tensor.transpose(flipped[:, u, :], words[:, u * P : (u + 1) * P], ident_f32[:])
            grouped = stage.tile([P, QUERIES * PACK], BF16, align_bytes=64, name="merged_grouped")
            nc.scalar.copy(
                out=grouped[:].bitcast(F32).rearrange("p (q u) -> p q u", u=WORD_PLANES),
                in_=flipped[:].rearrange("p u q -> p q u"),
            )
            merged_grouped[half] = grouped

        def project(w, g, tiles):
            m_codes, m_scales = merged_mx[w * PASSES + g]
            for first, width in tiles:
                if g == 0:
                    out_banks[w, first] = psum_turns.tile([P, N_TILE], F32, tag="turn", name="out_bank")
                nc.tensor.matmul_mx(
                    out=out_banks[w, first][:, :width],
                    lhsT=m_codes[:].bitcast(FP8X4),
                    lhsT_scale=m_scales[:],
                    rhs=w_words[:, g, first * PACK : (first + width) * PACK].bitcast(FP8X4),
                    rhs_scale=w_scales[:, g, first : first + width],
                    start=(g == 0),
                    stop=(g == PASSES - 1),
                )

        def finish(w, tiles):
            for first, width in tiles:
                cols = slice(first, first + width)
                result = results.tile([P, N_TILE], F32)
                nc.vector.tensor_add(out=result[:, :width], in0=out_banks[w, first][:, :width], in1=bias_all[:, cols])
                nc.sync.dma_start(out=out_rows[w][:, cols], in_=result[:, :width])

        LEFT, RIGHT = [(0, N_TILE)], [(N_TILE, N_TILE)]

        def half_closed_by(j):
            if 0 <= j < GROUPS and j % GROUPS_PER_HALF == GROUPS_PER_HALF - 1:
                return j // GROUPS_PER_HALF
            return None

        LAST = HALVES - 1
        for i in range(GROUPS - 1):
            to_transpose, to_quantise = half_closed_by(i - 3), half_closed_by(i - 4)
            if i >= 3:
                round_mixed(i - 3)
            if i >= 1:
                regroup_v(i - 1)
                quantise_attn(i - 1)
                quantise_v(i - 1)
            if to_quantise is not None:
                quantise_merged(to_quantise)
            transpose_attn(i)
            if to_transpose is not None:
                transpose_merged(to_transpose)
            if i >= 2:
                mix_values(i - 2)
            if i == 1:
                spread_bias()
        regroup_v(10)
        quantise_attn(10)
        quantise_v(10)
        round_mixed(8)
        transpose_attn(11, 2, 0)
        transpose_attn(11, 2, 2)
        mix_values(9)
        round_mixed(9)
        mix_values(10)
        quantise_attn(11, 2, 0)
        regroup_v(11)
        quantise_attn(11, 2, 2)
        quantise_v(11)
        quantise_merged(3)
        transpose_merged(4)
        round_mixed(10)
        quantise_merged(4)
        project(0, 0, LEFT)
        project(0, 1, LEFT)
        mix_values(11)
        finish(0, LEFT)
        round_mixed(11)
        project(1, 0, LEFT)
        project(1, 1, LEFT)
        finish(1, LEFT)
        transpose_merged(LAST)
        project(0, 0, RIGHT)
        project(0, 1, RIGHT)
        quantise_merged(LAST)
        finish(0, RIGHT)
        project(1, 0, RIGHT)
        project(1, 1, RIGHT)
        finish(1, RIGHT)
        project(2, 0, LEFT + RIGHT)
        project(2, 1, LEFT + RIGHT)
        finish(2, LEFT + RIGHT)
